import numpy as np
import ml_dtypes


def mxq(x, axis, fmt="e4m3"):
    dtype, down = {"e4m3": (ml_dtypes.float8_e4m3fn, 7), "e5m2": (ml_dtypes.float8_e5m2, 14)}[fmt]
    v = np.moveaxis(np.asarray(x, np.float32).astype(ml_dtypes.bfloat16).astype(np.float64), axis, -1)
    blocks = v.reshape(v.shape[:-1] + (-1, 32))
    amax = np.abs(blocks).max(-1, keepdims=True)
    byte = np.maximum(np.where(amax > 0, np.frexp(amax)[1] - 1 + 127, 0) - down, 1)
    scale = np.exp2(byte - 127.0)
    codes = (blocks / scale).astype(np.float32).astype(dtype).astype(np.float64)
    return np.moveaxis((codes * scale).reshape(v.shape), -1, axis)


WIDE = False


def mx_kscale(k):
    if not WIDE:
        return np.ones(k)
    levels = np.array([10, -10, 5, -5, 0])
    if k % 512:
        return np.exp2(np.random.permutation(np.resize(levels, k // 32))).repeat(32)
    a = np.empty((k // 512, 16))
    for p in range(k // 512):
        a[p, :8] = np.random.permutation(np.resize(levels, 8))
        for g in range(8):
            far = levels[np.abs(levels - a[p, g]) >= 10]
            a[p, g + 8] = far[np.random.randint(len(far))]
    return np.exp2(a.ravel()).repeat(32)


BF16 = ml_dtypes.bfloat16


def bf(x):
    return np.asarray(x, np.float32).astype(BF16)


def f64(x):
    return np.asarray(x).astype(np.float64)


B, S, D, H, HD, M, G = 4, 128, 1024, 8, 128, 4096, 3
EPS = 1e-6
HH = H * HD


def silu(v):
    return v / (1.0 + np.exp(-v))


def rmsnorm(x, gain):
    var = np.mean(np.square(x), axis=-1, keepdims=True)
    return x * (1.0 / np.sqrt(var + EPS)) * gain


def setup_inputs():
    s, t = mx_kscale(HH), mx_kscale(D)
    return {"attn": bf(0.3 * np.random.standard_normal((B, S, HH)) * s),
            "x": bf(np.random.standard_normal((B, S, D))),
            "w_o": bf(np.random.standard_normal((HH, D)) * 2.0 / np.sqrt(HH) / s[:, None]),
            "rms2_scale": bf((1.0 + 0.1 * np.random.standard_normal(D)) * t),
            "w_gate": bf(np.random.standard_normal((D, M)) / np.sqrt(D) / t[:, None]),
            "w_up": bf(np.random.standard_normal((D, M)) / np.sqrt(D) / t[:, None])}


def reference(attn, x, w_o, rms2_scale, w_gate, w_up):
    x_mid = f64(x) + (mxq(f64(attn), 2, "e4m3") @ mxq(f64(w_o), 0, "e4m3"))
    hq = mxq(rmsnorm(x_mid, f64(rms2_scale)), 2, "e4m3")
    g = silu(hq @ mxq(f64(w_gate), 0, "e4m3")) * (hq @ mxq(f64(w_up), 0, "e4m3"))
    return x_mid, g

@@ -1,0 +1,347 @@
+from contextlib import ExitStack
+
+import concourse.mybir as mybir
+from concourse.masks import make_identity
+
+F32 = mybir.dt.float32
+BF16 = mybir.dt.bfloat16
+U32 = mybir.dt.uint32
+U8 = mybir.dt.uint8
+FP8X4 = mybir.dt.float8_e4m3fn_x4
+ACT = mybir.ActivationFunctionType
+ALU = mybir.AluOpType
+
+P = 128
+PACK = 4
+K_PASS = P * PACK
+TOKENS = 512
+D_MODEL = 1024
+D_FF = 4096
+TOKEN_TILES = TOKENS // P
+PASSES = D_MODEL // K_PASS
+N_TILE = 512
+HALVES = D_MODEL // N_TILE
+CHUNKS = D_FF // N_TILE
+STEPS = CHUNKS * TOKEN_TILES
+LOAD_COLS = 2 * N_TILE
+UNITS = 2 * PASSES * (D_FF // LOAD_COLS)
+RAW_BUFS = 9
+PARTS = 4
+PIECE = N_TILE // 2
+LEAD = 7
+RUN = 4
+GATE, UP = 0, 1
+EPS = 1e-6
+
+FLOPS = 2 * TOKENS * D_MODEL * (D_MODEL + 2 * D_FF)
+
+
+def regroup(copy, grouped_cols, raw_cols):
+    copy(
+        out=grouped_cols.rearrange("p (c i) t -> p c t i", i=RUN),
+        in_=raw_cols.rearrange("p t (c i) -> p c t i", i=RUN),
+    )
+
+
+def tile_transformerblocktpu_pb_kernel(
+    tc, attn, x, w_o, rms2_scale, w_gate, w_up, out_0, out_1
+):
+    nc = tc.nc
+    attn_rows = attn.flatten_outer_dims()
+    x_rows = x.flatten_outer_dims()
+    xmid_rows = out_0.flatten_outer_dims()
+    g_rows = out_1.flatten_outer_dims()
+
+    with ExitStack() as ctx:
+        consts = ctx.enter_context(tc.tile_pool(name="consts", bufs=1))
+        keep = ctx.enter_context(tc.tile_pool(name="keep", bufs=1))
+        raw_pool = ctx.enter_context(tc.tile_pool(name="raw", bufs=RAW_BUFS))
+        stage = ctx.enter_context(tc.tile_pool(name="stage", bufs=3))
+        rows = ctx.enter_context(tc.tile_pool(name="rows", bufs=2))
+        codes_pool = ctx.enter_context(tc.tile_pool(name="codes", bufs=3))
+        ep = ctx.enter_context(tc.tile_pool(name="ep", bufs=3))
+        out_pool = ctx.enter_context(tc.tile_pool(name="out", bufs=8))
+        banks = ctx.enter_context(tc.psum_pool(name="banks", bufs=8))
+        ctx.enter_context(tc.manual_schedule())
+
+        raws = {}
+        grouped = {}
+        w_codes = {}
+        w_scales = {}
+
+        def load_unit(unit):
+            pair, rest = divmod(unit, 2 * PASSES)
+            m, g = divmod(rest, PASSES)
+            w = (w_gate, w_up)[m]
+            raw = raw_pool.tile([P, PACK, LOAD_COLS], BF16, tag="raw")
+            nc.sync.dma_start(
+                out=raw[:],
+                in_=w[
+                    g * K_PASS : (g + 1) * K_PASS, pair * LOAD_COLS : (pair + 1) * LOAD_COLS
+                ].rearrange("(p t) n -> p t n", t=PACK),
+            )
+            raws[unit] = raw
+
+        def raw_cols(chunk, m, g, first, width):
+            start = (chunk % 2) * N_TILE + first
+            unit = (chunk // 2) * 2 * PASSES + m * PASSES + g
+            return raws[unit][:, :, start : start + width]
+
+        def quantise(chunk, m, g):
+            nc.vector.quantize_mx(
+                out=w_codes[chunk][:, m, g, :].bitcast(FP8X4),
+                scales=w_scales[chunk][:, m, g, :],
+                in_=grouped[(chunk, m, g)][:].rearrange("p n t -> p (n t)"),
+            )
+
+        def scalar_regroup(index):
+            chunk, piece = divmod(index, PARTS)
+            if chunk < CHUNKS:
+                m, side = divmod(piece, 2)
+                if side == 0:
+                    by_scalar = stage.tile([P, N_TILE, PACK], BF16, align_bytes=64)
+                    grouped[(chunk, m, 1)] = by_scalar
+                first = side * PIECE
+                regroup(
+                    nc.scalar.copy,
+                    grouped[(chunk, m, 1)][:, first : first + PIECE, :],
+                    raw_cols(chunk, m, 1, first, PIECE),
+                )
+
+        def vector_prepare(index):
+            chunk, part = divmod(index, PARTS)
+            if chunk < CHUNKS:
+                if part < 2:
+                    by_vector = stage.tile([P, N_TILE, PACK], BF16, align_bytes=64)
+                    regroup(nc.vector.tensor_copy, by_vector[:], raw_cols(chunk, part, 0, 0, N_TILE))
+                    grouped[(chunk, part, 0)] = by_vector
+                if part == 2:
+                    codes = codes_pool.tile([P, 2, PASSES, N_TILE], U32, align_bytes=64)
+                    scales = codes_pool.tile([P, 2, PASSES, N_TILE], U8, align_bytes=64)
+                    w_codes[chunk] = codes
+                    w_scales[chunk] = scales
+                    quantise(chunk, GATE, 0)
+                    quantise(chunk, UP, 0)
+                if part == 3:
+                    quantise(chunk, GATE, 1)
+                    quantise(chunk, UP, 1)
+                    if chunk % 2 == 1:
+                        freed = (chunk // 2) * 2 * PASSES
+                        for unit in range(freed + RAW_BUFS, min(freed + RAW_BUFS + 4, UNITS)):
+                            load_unit(unit)
+
+        gain_row = consts.tile([P, D_MODEL], BF16)
+        nc.vector.memset(gain_row[:], 0.0)
+        neg_half = consts.tile([P, 1], F32)
+        nc.vector.memset(neg_half[:], -0.5)
+        ones = consts.tile([P, P], BF16)
+        nc.vector.memset(ones[:], 1.0)
+        warm = consts.tile([P, 1], F32)
+        nc.scalar.activation(out=warm[:], in_=neg_half[:], func=ACT.Silu)
+        ident_f32 = consts.tile([P, P], F32)
+        make_identity(nc, ident_f32[:])
+
+        wo_raw = []
+        for g in range(PASSES):
+            raw = raw_pool.tile([P, PACK, LOAD_COLS], BF16, tag="raw")
+            nc.sync.dma_start(
+                out=raw[:],
+                in_=w_o[g * K_PASS : (g + 1) * K_PASS, :].rearrange("(p t) n -> p t n", t=PACK),
+            )
+            wo_raw.append(raw)
+            if g == 0:
+                nc.sync.dma_start(out=gain_row[0:1, :], in_=rms2_scale.unsqueeze(0))
+        attn_sb = keep.tile([P, TOKEN_TILES, D_MODEL], BF16)
+        for i in range(TOKEN_TILES):
+            nc.sync.dma_start(out=attn_sb[:, i, :], in_=attn_rows[i * P : (i + 1) * P, :])
+        x_sb = keep.tile([P, TOKEN_TILES, D_MODEL], BF16)
+        for i in range(TOKEN_TILES):
+            nc.sync.dma_start(out=x_sb[:, i, :], in_=x_rows[i * P : (i + 1) * P, :])
+        for unit in range(RAW_BUFS):
+            load_unit(unit)
+
+        gain_banks = []
+        for half in range(HALVES):
+            gain_ps = banks.tile([P, N_TILE], F32, tag="bank")
+            nc.tensor.matmul(
+                out=gain_ps[:],
+                lhsT=ones[:],
+                rhs=gain_row[:, half * N_TILE : (half + 1) * N_TILE],
+                start=True,
+                stop=True,
+            )
+            gain_banks.append(gain_ps)
+
+        wo_codes = keep.tile([P, PASSES, D_MODEL], U32, align_bytes=64)
+        wo_scales = keep.tile([P, PASSES, D_MODEL], U8, align_bytes=64)
+        for g in range(PASSES):
+            by_vector = stage.tile([P, N_TILE, PACK], BF16, align_bytes=64)
+            regroup(nc.vector.tensor_copy, by_vector[:], wo_raw[g][:, :, 0:N_TILE])
+            by_scalar = stage.tile([P, N_TILE, PACK], BF16, align_bytes=64)
+            regroup(nc.scalar.copy, by_scalar[:], wo_raw[g][:, :, N_TILE : 2 * N_TILE])
+            for half, tile_ in enumerate((by_vector, by_scalar)):
+                cols = slice(half * N_TILE, (half + 1) * N_TILE)
+                nc.vector.quantize_mx(
+                    out=wo_codes[:, g, cols].bitcast(FP8X4),
+                    scales=wo_scales[:, g, cols],
+                    in_=tile_[:].rearrange("p n t -> p (n t)"),
+                )
+
+        a_grouped = keep.tile([P, TOKEN_TILES, PASSES, P, PACK], BF16, align_bytes=64)
+        a_codes = keep.tile([P, TOKEN_TILES, PASSES, P], U32, align_bytes=64)
+        a_scales = keep.tile([P, TOKEN_TILES, PASSES, P], U8, align_bytes=64)
+        for i in range(TOKEN_TILES):
+            attn_words = attn_sb[:, i, :].bitcast(F32)
+            at = banks.tile([P, PASSES, 2, P], F32, tag="bank")
+            for g in range(PASSES):
+                for u in range(2):
+                    nc.tensor.transpose(
+                        out=at[:, g, u, :],
+                        in_=attn_words[:, 2 * P * g + u : 2 * P * (g + 1) : 2],
+                        identity=ident_f32[:],
+                    )
+            nc.scalar.copy(
+                out=a_grouped[:, i].bitcast(F32),
+                in_=at[:].rearrange("q g u r -> q g r u"),
+            )
+            nc.vector.quantize_mx(
+                out=a_codes[:, i].rearrange("q g r -> q (g r)").bitcast(FP8X4),
+                scales=a_scales[:, i].rearrange("q g r -> q (g r)"),
+                in_=a_grouped[:, i].rearrange("q g r t -> q (g r t)"),
+            )
+
+        gain_all = consts.tile([P, D_MODEL], BF16)
+        for half in range(HALVES):
+            nc.scalar.mul(
+                out=gain_all[:, half * N_TILE : (half + 1) * N_TILE],
+                in_=gain_banks[half][:],
+                mul=D_MODEL**0.5,
+            )
+
+        xmid = keep.tile([P, TOKEN_TILES, D_MODEL], F32)
+        sumsq = keep.tile([P, TOKEN_TILES], F32)
+        shifted = keep.tile([P, TOKEN_TILES], F32)
+        inv_norm = keep.tile([P, TOKEN_TILES], F32)
+        h_codes = keep.tile([P, TOKEN_TILES, PASSES, P], U32, align_bytes=64)
+        h_scales = keep.tile([P, TOKEN_TILES, PASSES, P], U8, align_bytes=64)
+        xm_banks = {}
+        h_groups = {}
+
+        def first_product(i):
+            for half in range(HALVES):
+                cols = slice(half * N_TILE, (half + 1) * N_TILE)
+                xm_ps = banks.tile([P, N_TILE], F32, tag="bank")
+                for g in range(PASSES):
+                    nc.tensor.matmul_mx(
+                        out=xm_ps[:],
+                        lhsT=a_codes[:, i, g, :].bitcast(FP8X4),
+                        lhsT_scale=a_scales[:, i, g, :],
+                        rhs=wo_codes[:, g, cols].bitcast(FP8X4),
+                        rhs_scale=wo_scales[:, g, cols],
+                        start=(g == 0),
+                        stop=(g == PASSES - 1),
+                    )
+                xm_banks[(i, half)] = xm_ps
+
+        def add_and_square(i):
+            one = slice(i, i + 1)
+            for half in range(HALVES):
+                cols = slice(half * N_TILE, (half + 1) * N_TILE)
+                nc.vector.tensor_tensor(
+                    out=xmid[:, i, cols], in0=xm_banks[(i, half)][:], in1=x_sb[:, i, cols], op=ALU.add
+                )
+            nc.sync.dma_start(out=xmid_rows[i * P : (i + 1) * P, :], in_=xmid[:, i, :])
+            squares = rows.tile([P, D_MODEL], BF16)
+            nc.scalar.activation(
+                out=squares[:], in_=xmid[:, i, :], func=ACT.Square, accum_out=sumsq[:, one]
+            )
+            nc.gpsimd.tensor_scalar(
+                out=shifted[:, one],
+                in0=sumsq[:, one],
+                scalar1=D_MODEL * EPS,
+                scalar2=1.0,
+                op0=ALU.add,
+                op1=ALU.mult,
+            )
+            nc.gpsimd.tensor_tensor(
+                out=inv_norm[:, one], in0=shifted[:, one], in1=neg_half[:], op=ALU.pow
+            )
+
+        def norm_and_transpose(i):
+            h_bf16 = rows.tile([P, D_MODEL], BF16)
+            nc.vector.scalar_tensor_tensor(
+                out=h_bf16[:],
+                in0=xmid[:, i, :],
+                scalar=inv_norm[:, i : i + 1],
+                in1=gain_all[:],
+                op0=ALU.mult,
+                op1=ALU.mult,
+            )
+            h_words = h_bf16[:].bitcast(F32)
+            ht = banks.tile([P, PASSES, 2, P], F32, tag="bank")
+            for g in range(PASSES):
+                for u in range(2):
+                    nc.tensor.transpose(
+                        out=ht[:, g, u, :],
+                        in_=h_words[:, 2 * P * g + u : 2 * P * (g + 1) : 2],
+                        identity=ident_f32[:],
+                    )
+            h_grouped = rows.tile([P, PASSES, P, PACK], BF16, align_bytes=64)
+            nc.scalar.copy(
+                out=h_grouped[:].rearrange("p g r t -> p (g r t)").bitcast(F32).rearrange(
+                    "q (g r u) -> q g r u", g=PASSES, u=2
+                ),
+                in_=ht[:].rearrange("q g u r -> q g r u"),
+            )
+            h_groups[i] = h_grouped
+
+        def quantise_h(i):
+            nc.vector.quantize_mx(
+                out=h_codes[:, i].rearrange("p g r -> p (g r)").bitcast(FP8X4),
+                scales=h_scales[:, i].rearrange("p g r -> p (g r)"),
+                in_=h_groups[i][:].rearrange("p g r t -> p (g r t)"),
+            )
+
+        for i in range(TOKEN_TILES):
+            first_product(i)
+            if i >= 1:
+                add_and_square(i - 1)
+        for i in range(TOKEN_TILES):
+            norm_and_transpose(i)
+            if i == 0:
+                add_and_square(TOKEN_TILES - 1)
+            vector_prepare(i)
+            if i >= 1:
+                quantise_h(i - 1)
+                scalar_regroup(2 * i - 1)
+            scalar_regroup(2 * i)
+        vector_prepare(TOKEN_TILES)
+        quantise_h(TOKEN_TILES - 1)
+        for index in range(TOKEN_TILES + 1, LEAD):
+            vector_prepare(index)
+
+        for step in range(STEPS):
+            chunk, i = divmod(step, TOKEN_TILES)
+            gate_ps = banks.tile([P, N_TILE], F32, tag="bank")
+            up_ps = banks.tile([P, N_TILE], F32, tag="bank")
+            for m, product in enumerate((gate_ps, up_ps)):
+                for g in range(PASSES):
+                    nc.tensor.matmul_mx(
+                        out=product[:],
+                        lhsT=h_codes[:, i, g, :].bitcast(FP8X4),
+                        lhsT_scale=h_scales[:, i, g, :],
+                        rhs=w_codes[chunk][:, m, g, :].bitcast(FP8X4),
+                        rhs_scale=w_scales[chunk][:, m, g, :],
+                        start=(g == 0),
+                        stop=(g == PASSES - 1),
+                    )
+            scalar_regroup(step + LEAD)
+            silu = ep.tile([P, N_TILE], F32)
+            nc.scalar.activation(out=silu[:], in_=gate_ps[:], func=ACT.Silu)
+            vector_prepare(step + LEAD)
+            g_sb = out_pool.tile([P, N_TILE], F32)
+            nc.vector.tensor_tensor(out=g_sb[:], in0=up_ps[:], in1=silu[:], op=ALU.mult)
+            first_col = chunk * N_TILE
+            nc.sync.dma_start(
+                out=g_rows[i * P : (i + 1) * P, first_col : first_col + N_TILE], in_=g_sb[:]
+            )

@@ -29,7 +29,7 @@ RAW_BUFS = 9
 PARTS = 4
 PIECE = N_TILE // 2
 LEAD = 7
-RUN = 4
+RUN = 8
 GATE, UP = 0, 1
 EPS = 1e-6
 

@@ -26,9 +26,12 @@ STEPS = CHUNKS * TOKEN_TILES
 LOAD_COLS = 2 * N_TILE
 UNITS = 2 * PASSES * (D_FF // LOAD_COLS)
 RAW_BUFS = 9
-PARTS = 4
-PIECE = N_TILE // 2
-LEAD = 7
+BEAT = 2
+BEATS = STEPS // BEAT
+LEAD = 3
+POOL_COLS = 192
+POOL_FIRST = 2
+HELP_COLS = 128
 RUN = 8
 GATE, UP = 0, 1
 EPS = 1e-6
@@ -56,12 +59,11 @@ def tile_transformerblocktpu_pb_kernel(
         consts = ctx.enter_context(tc.tile_pool(name="consts", bufs=1))
         keep = ctx.enter_context(tc.tile_pool(name="keep", bufs=1))
         raw_pool = ctx.enter_context(tc.tile_pool(name="raw", bufs=RAW_BUFS))
-        stage = ctx.enter_context(tc.tile_pool(name="stage", bufs=3))
+        stage = ctx.enter_context(tc.tile_pool(name="stage", bufs=2))
         rows = ctx.enter_context(tc.tile_pool(name="rows", bufs=2))
         codes_pool = ctx.enter_context(tc.tile_pool(name="codes", bufs=3))
-        ep = ctx.enter_context(tc.tile_pool(name="ep", bufs=3))
-        out_pool = ctx.enter_context(tc.tile_pool(name="out", bufs=8))
-        banks = ctx.enter_context(tc.psum_pool(name="banks", bufs=8))
+        ep = ctx.enter_context(tc.tile_pool(name="ep", bufs=4))
+        out_pool = ctx.enter_context(tc.tile_pool(name="out", bufs=12))
         ctx.enter_context(tc.manual_schedule())
 
         raws = {}
@@ -94,41 +96,86 @@ def tile_transformerblocktpu_pb_kernel(
                 in_=grouped[(chunk, m, g)][:].rearrange("p n t -> p (n t)"),
             )
 
-        def scalar_regroup(index):
-            chunk, piece = divmod(index, PARTS)
+        def block(chunk, m, g, bufs):
+            if (chunk, m, g) not in grouped:
+                whole = stage.tile(
+                    [P, N_TILE, PACK], BF16, tag="block%d%d" % (m, g), bufs=bufs, align_bytes=64
+                )
+                grouped[(chunk, m, g)] = whole
+            return grouped[(chunk, m, g)]
+
+        def pool_cols(chunk):
+            return POOL_COLS if chunk >= POOL_FIRST else 0
+
+        def vector_regroup(chunk, m):
             if chunk < CHUNKS:
-                m, side = divmod(piece, 2)
-                if side == 0:
-                    by_scalar = stage.tile([P, N_TILE, PACK], BF16, align_bytes=64)
-                    grouped[(chunk, m, 1)] = by_scalar
-                first = side * PIECE
+                first = pool_cols(chunk) + HELP_COLS if m == UP else 0
                 regroup(
-                    nc.scalar.copy,
-                    grouped[(chunk, m, 1)][:, first : first + PIECE, :],
-                    raw_cols(chunk, m, 1, first, PIECE),
+                    nc.vector.tensor_copy,
+                    block(chunk, m, 0, 1 if m == UP else 2)[:, first:, :],
+                    raw_cols(chunk, m, 0, first, N_TILE - first),
                 )
 
-        def vector_prepare(index):
-            chunk, part = divmod(index, PARTS)
+        def scalar_regroup(chunk, m):
             if chunk < CHUNKS:
-                if part < 2:
-                    by_vector = stage.tile([P, N_TILE, PACK], BF16, align_bytes=64)
-                    regroup(nc.vector.tensor_copy, by_vector[:], raw_cols(chunk, part, 0, 0, N_TILE))
-                    grouped[(chunk, part, 0)] = by_vector
-                if part == 2:
-                    codes = codes_pool.tile([P, 2, PASSES, N_TILE], U32, align_bytes=64)
-                    scales = codes_pool.tile([P, 2, PASSES, N_TILE], U8, align_bytes=64)
-                    w_codes[chunk] = codes
-                    w_scales[chunk] = scales
-                    quantise(chunk, GATE, 0)
-                    quantise(chunk, UP, 0)
-                if part == 3:
-                    quantise(chunk, GATE, 1)
-                    quantise(chunk, UP, 1)
-                    if chunk % 2 == 1:
-                        freed = (chunk // 2) * 2 * PASSES
-                        for unit in range(freed + RAW_BUFS, min(freed + RAW_BUFS + 4, UNITS)):
-                            load_unit(unit)
+                first = pool_cols(chunk) if m == UP else 0
+                regroup(
+                    nc.scalar.copy,
+                    block(chunk, m, 1, 1 if m == UP else 2)[:, first:, :],
+                    raw_cols(chunk, m, 1, first, N_TILE - first),
+                )
+
+        def scalar_help(chunk):
+            if chunk < CHUNKS:
+                first = pool_cols(chunk)
+                regroup(
+                    nc.scalar.copy,
+                    block(chunk, UP, 0, 1)[:, first : first + HELP_COLS, :],
+                    raw_cols(chunk, UP, 0, first, HELP_COLS),
+                )
+
+        def pool_regroup(chunk, g):
+            if POOL_FIRST <= chunk < CHUNKS:
+                nc.gpsimd.tensor_scalar(
+                    out=block(chunk, UP, g, 1)[:, 0:POOL_COLS, :],
+                    in0=raw_cols(chunk, UP, g, 0, POOL_COLS).rearrange("p t n -> p n t"),
+                    scalar1=1.0,
+                    scalar2=0.0,
+                    op0=ALU.mult,
+                    op1=ALU.add,
+                )
+
+        def quantise_pass(chunk, g):
+            if g == 0:
+                codes = codes_pool.tile([P, 2, PASSES, N_TILE], U32, align_bytes=64)
+                scales = codes_pool.tile([P, 2, PASSES, N_TILE], U8, align_bytes=64)
+                w_codes[chunk] = codes
+                w_scales[chunk] = scales
+            quantise(chunk, GATE, g)
+            quantise(chunk, UP, g)
+
+        def refill(first, count):
+            for unit in range(first, min(first + count, UNITS)):
+                load_unit(unit)
+
+        def scalar_prepare(beat):
+            chunk, g = divmod(beat, 2)
+            if g == 0:
+                scalar_regroup(chunk, UP)
+            else:
+                scalar_help(chunk + 1)
+                scalar_regroup(chunk + 1, GATE)
+
+        def vector_prepare(beat):
+            chunk, g = divmod(beat, 2)
+            if chunk < CHUNKS:
+                vector_regroup(chunk + 1, UP if g else GATE)
+                quantise_pass(chunk, g)
+                pool_regroup(chunk + 1, g)
+                if chunk % 2 == 0 and g == 1:
+                    refill(chunk // 2 * 2 * PASSES + RAW_BUFS, 3)
+                if chunk % 2 == 1 and g == 0:
+                    refill(chunk // 2 * 2 * PASSES + RAW_BUFS + 3, 1)
 
         gain_row = consts.tile([P, D_MODEL], BF16)
         nc.vector.memset(gain_row[:], 0.0)
@@ -160,188 +207,195 @@ def tile_transformerblocktpu_pb_kernel(
         for unit in range(RAW_BUFS):
             load_unit(unit)
 
-        gain_banks = []
-        for half in range(HALVES):
-            gain_ps = banks.tile([P, N_TILE], F32, tag="bank")
-            nc.tensor.matmul(
-                out=gain_ps[:],
-                lhsT=ones[:],
-                rhs=gain_row[:, half * N_TILE : (half + 1) * N_TILE],
-                start=True,
-                stop=True,
-            )
-            gain_banks.append(gain_ps)
+        with ExitStack() as head:
+            head_banks = head.enter_context(tc.psum_pool(name="head_banks", bufs=7))
+            gain_bank = head.enter_context(tc.psum_pool(name="gain_bank", bufs=1))
+            gain_ps = gain_bank.tile([P, D_MODEL], BF16)
+            for half in range(HALVES):
+                nc.tensor.matmul(
+                    out=gain_ps[:, half * N_TILE : (half + 1) * N_TILE],
+                    lhsT=ones[:],
+                    rhs=gain_row[:, half * N_TILE : (half + 1) * N_TILE],
+                    start=True,
+                    stop=True,
+                )
 
-        wo_codes = keep.tile([P, PASSES, D_MODEL], U32, align_bytes=64)
-        wo_scales = keep.tile([P, PASSES, D_MODEL], U8, align_bytes=64)
-        for g in range(PASSES):
-            by_vector = stage.tile([P, N_TILE, PACK], BF16, align_bytes=64)
-            regroup(nc.vector.tensor_copy, by_vector[:], wo_raw[g][:, :, 0:N_TILE])
-            by_scalar = stage.tile([P, N_TILE, PACK], BF16, align_bytes=64)
-            regroup(nc.scalar.copy, by_scalar[:], wo_raw[g][:, :, N_TILE : 2 * N_TILE])
-            for half, tile_ in enumerate((by_vector, by_scalar)):
-                cols = slice(half * N_TILE, (half + 1) * N_TILE)
+            wo_codes = keep.tile([P, PASSES, D_MODEL], U32, align_bytes=64)
+            wo_scales = keep.tile([P, PASSES, D_MODEL], U8, align_bytes=64)
+            for g in range(PASSES):
+                by_vector = stage.tile([P, N_TILE, PACK], BF16, tag="block00", align_bytes=64)
+                regroup(nc.vector.tensor_copy, by_vector[:], wo_raw[g][:, :, 0:N_TILE])
+                by_scalar = stage.tile([P, N_TILE, PACK], BF16, tag="block01", align_bytes=64)
+                regroup(nc.scalar.copy, by_scalar[:], wo_raw[g][:, :, N_TILE : 2 * N_TILE])
+                for half, tile_ in enumerate((by_vector, by_scalar)):
+                    cols = slice(half * N_TILE, (half + 1) * N_TILE)
+                    nc.vector.quantize_mx(
+                        out=wo_codes[:, g, cols].bitcast(FP8X4),
+                        scales=wo_scales[:, g, cols],
+                        in_=tile_[:].rearrange("p n t -> p (n t)"),
+                    )
+
+            a_grouped = keep.tile([P, TOKEN_TILES, PASSES, P, PACK], BF16, align_bytes=64)
+            a_codes = keep.tile([P, TOKEN_TILES, PASSES, P], U32, align_bytes=64)
+            a_scales = keep.tile([P, TOKEN_TILES, PASSES, P], U8, align_bytes=64)
+            for i in range(TOKEN_TILES):
+                attn_words = attn_sb[:, i, :].bitcast(F32)
+                at = head_banks.tile([P, PASSES, 2, P], F32, tag="bank")
+                for g in range(PASSES):
+                    for u in range(2):
+                        nc.tensor.transpose(
+                            out=at[:, g, u, :],
+                            in_=attn_words[:, 2 * P * g + u : 2 * P * (g + 1) : 2],
+                            identity=ident_f32[:],
+                        )
+                nc.scalar.copy(
+                    out=a_grouped[:, i].bitcast(F32),
+                    in_=at[:].rearrange("q g u r -> q g r u"),
+                )
                 nc.vector.quantize_mx(
-                    out=wo_codes[:, g, cols].bitcast(FP8X4),
-                    scales=wo_scales[:, g, cols],
-                    in_=tile_[:].rearrange("p n t -> p (n t)"),
+                    out=a_codes[:, i].rearrange("q g r -> q (g r)").bitcast(FP8X4),
+                    scales=a_scales[:, i].rearrange("q g r -> q (g r)"),
+                    in_=a_grouped[:, i].rearrange("q g r t -> q (g r t)"),
                 )
 
-        a_grouped = keep.tile([P, TOKEN_TILES, PASSES, P, PACK], BF16, align_bytes=64)
-        a_codes = keep.tile([P, TOKEN_TILES, PASSES, P], U32, align_bytes=64)
-        a_scales = keep.tile([P, TOKEN_TILES, PASSES, P], U8, align_bytes=64)
-        for i in range(TOKEN_TILES):
-            attn_words = attn_sb[:, i, :].bitcast(F32)
-            at = banks.tile([P, PASSES, 2, P], F32, tag="bank")
-            for g in range(PASSES):
-                for u in range(2):
-                    nc.tensor.transpose(
-                        out=at[:, g, u, :],
-                        in_=attn_words[:, 2 * P * g + u : 2 * P * (g + 1) : 2],
-                        identity=ident_f32[:],
+            xmid = keep.tile([P, TOKEN_TILES, D_MODEL], F32)
+            sumsq = keep.tile([P, TOKEN_TILES], F32)
+            shifted = keep.tile([P, TOKEN_TILES], F32)
+            inv_norm = keep.tile([P, TOKEN_TILES], F32)
+            h_codes = keep.tile([P, TOKEN_TILES, PASSES, P], U32, align_bytes=64)
+            h_scales = keep.tile([P, TOKEN_TILES, PASSES, P], U8, align_bytes=64)
+            xm_banks = {}
+            h_groups = {}
+
+            def first_product(i):
+                for half in range(HALVES):
+                    cols = slice(half * N_TILE, (half + 1) * N_TILE)
+                    xm_ps = head_banks.tile([P, N_TILE], F32, tag="bank")
+                    for g in range(PASSES):
+                        nc.tensor.matmul_mx(
+                            out=xm_ps[:],
+                            lhsT=a_codes[:, i, g, :].bitcast(FP8X4),
+                            lhsT_scale=a_scales[:, i, g, :],
+                            rhs=wo_codes[:, g, cols].bitcast(FP8X4),
+                            rhs_scale=wo_scales[:, g, cols],
+                            start=(g == 0),
+                            stop=(g == PASSES - 1),
+                        )
+                    xm_banks[(i, half)] = xm_ps
+
+            def add_and_square(i):
+                one = slice(i, i + 1)
+                for half in range(HALVES):
+                    cols = slice(half * N_TILE, (half + 1) * N_TILE)
+                    nc.vector.tensor_tensor(
+                        out=xmid[:, i, cols], in0=xm_banks[(i, half)][:], in1=x_sb[:, i, cols], op=ALU.add
                     )
-            nc.scalar.copy(
-                out=a_grouped[:, i].bitcast(F32),
-                in_=at[:].rearrange("q g u r -> q g r u"),
-            )
-            nc.vector.quantize_mx(
-                out=a_codes[:, i].rearrange("q g r -> q (g r)").bitcast(FP8X4),
-                scales=a_scales[:, i].rearrange("q g r -> q (g r)"),
-                in_=a_grouped[:, i].rearrange("q g r t -> q (g r t)"),
-            )
-
-        gain_all = consts.tile([P, D_MODEL], BF16)
-        for half in range(HALVES):
-            nc.scalar.mul(
-                out=gain_all[:, half * N_TILE : (half + 1) * N_TILE],
-                in_=gain_banks[half][:],
-                mul=D_MODEL**0.5,
-            )
-
-        xmid = keep.tile([P, TOKEN_TILES, D_MODEL], F32)
-        sumsq = keep.tile([P, TOKEN_TILES], F32)
-        shifted = keep.tile([P, TOKEN_TILES], F32)
-        inv_norm = keep.tile([P, TOKEN_TILES], F32)
-        h_codes = keep.tile([P, TOKEN_TILES, PASSES, P], U32, align_bytes=64)
-        h_scales = keep.tile([P, TOKEN_TILES, PASSES, P], U8, align_bytes=64)
-        xm_banks = {}
-        h_groups = {}
-
-        def first_product(i):
-            for half in range(HALVES):
-                cols = slice(half * N_TILE, (half + 1) * N_TILE)
-                xm_ps = banks.tile([P, N_TILE], F32, tag="bank")
-                for g in range(PASSES):
-                    nc.tensor.matmul_mx(
-                        out=xm_ps[:],
-                        lhsT=a_codes[:, i, g, :].bitcast(FP8X4),
-                        lhsT_scale=a_scales[:, i, g, :],
-                        rhs=wo_codes[:, g, cols].bitcast(FP8X4),
-                        rhs_scale=wo_scales[:, g, cols],
-                        start=(g == 0),
-                        stop=(g == PASSES - 1),
-                    )
-                xm_banks[(i, half)] = xm_ps
-
-        def add_and_square(i):
-            one = slice(i, i + 1)
-            for half in range(HALVES):
-                cols = slice(half * N_TILE, (half + 1) * N_TILE)
-                nc.vector.tensor_tensor(
-                    out=xmid[:, i, cols], in0=xm_banks[(i, half)][:], in1=x_sb[:, i, cols], op=ALU.add
+                nc.sync.dma_start(out=xmid_rows[i * P : (i + 1) * P, :], in_=xmid[:, i, :])
+                squares = rows.tile([P, D_MODEL], BF16)
+                nc.scalar.activation(
+                    out=squares[:], in_=xmid[:, i, :], func=ACT.Square, accum_out=sumsq[:, one]
                 )
-            nc.sync.dma_start(out=xmid_rows[i * P : (i + 1) * P, :], in_=xmid[:, i, :])
-            squares = rows.tile([P, D_MODEL], BF16)
-            nc.scalar.activation(
-                out=squares[:], in_=xmid[:, i, :], func=ACT.Square, accum_out=sumsq[:, one]
-            )
-            nc.gpsimd.tensor_scalar(
-                out=shifted[:, one],
-                in0=sumsq[:, one],
-                scalar1=D_MODEL * EPS,
-                scalar2=1.0,
-                op0=ALU.add,
-                op1=ALU.mult,
-            )
-            nc.gpsimd.tensor_tensor(
-                out=inv_norm[:, one], in0=shifted[:, one], in1=neg_half[:], op=ALU.pow
-            )
+                nc.gpsimd.tensor_scalar(
+                    out=shifted[:, one],
+                    in0=sumsq[:, one],
+                    scalar1=D_MODEL * EPS,
+                    scalar2=1.0 / D_MODEL,
+                    op0=ALU.add,
+                    op1=ALU.mult,
+                )
+                nc.gpsimd.tensor_tensor(
+                    out=inv_norm[:, one], in0=shifted[:, one], in1=neg_half[:], op=ALU.pow
+                )
 
-        def norm_and_transpose(i):
-            h_bf16 = rows.tile([P, D_MODEL], BF16)
-            nc.vector.scalar_tensor_tensor(
-                out=h_bf16[:],
-                in0=xmid[:, i, :],
-                scalar=inv_norm[:, i : i + 1],
-                in1=gain_all[:],
-                op0=ALU.mult,
-                op1=ALU.mult,
-            )
-            h_words = h_bf16[:].bitcast(F32)
-            ht = banks.tile([P, PASSES, 2, P], F32, tag="bank")
-            for g in range(PASSES):
-                for u in range(2):
-                    nc.tensor.transpose(
-                        out=ht[:, g, u, :],
-                        in_=h_words[:, 2 * P * g + u : 2 * P * (g + 1) : 2],
-                        identity=ident_f32[:],
-                    )
-            h_grouped = rows.tile([P, PASSES, P, PACK], BF16, align_bytes=64)
-            nc.scalar.copy(
-                out=h_grouped[:].rearrange("p g r t -> p (g r t)").bitcast(F32).rearrange(
-                    "q (g r u) -> q g r u", g=PASSES, u=2
-                ),
-                in_=ht[:].rearrange("q g u r -> q g r u"),
-            )
-            h_groups[i] = h_grouped
-
-        def quantise_h(i):
-            nc.vector.quantize_mx(
-                out=h_codes[:, i].rearrange("p g r -> p (g r)").bitcast(FP8X4),
-                scales=h_scales[:, i].rearrange("p g r -> p (g r)"),
-                in_=h_groups[i][:].rearrange("p g r t -> p (g r t)"),
-            )
-
-        for i in range(TOKEN_TILES):
-            first_product(i)
-            if i >= 1:
-                add_and_square(i - 1)
-        for i in range(TOKEN_TILES):
-            norm_and_transpose(i)
-            if i == 0:
-                add_and_square(TOKEN_TILES - 1)
-            vector_prepare(i)
-            if i >= 1:
-                quantise_h(i - 1)
-                scalar_regroup(2 * i - 1)
-            scalar_regroup(2 * i)
-        vector_prepare(TOKEN_TILES)
-        quantise_h(TOKEN_TILES - 1)
-        for index in range(TOKEN_TILES + 1, LEAD):
-            vector_prepare(index)
-
-        for step in range(STEPS):
-            chunk, i = divmod(step, TOKEN_TILES)
-            gate_ps = banks.tile([P, N_TILE], F32, tag="bank")
-            up_ps = banks.tile([P, N_TILE], F32, tag="bank")
-            for m, product in enumerate((gate_ps, up_ps)):
+            def norm_and_transpose(i):
+                h_bf16 = rows.tile([P, D_MODEL], BF16)
+                nc.vector.scalar_tensor_tensor(
+                    out=h_bf16[:],
+                    in0=xmid[:, i, :],
+                    scalar=inv_norm[:, i : i + 1],
+                    in1=gain_ps[:],
+                    op0=ALU.mult,
+                    op1=ALU.mult,
+                )
+                h_words = h_bf16[:].bitcast(F32)
+                ht = head_banks.tile([P, PASSES, 2, P], F32, tag="bank")
                 for g in range(PASSES):
-                    nc.tensor.matmul_mx(
-                        out=product[:],
-                        lhsT=h_codes[:, i, g, :].bitcast(FP8X4),
-                        lhsT_scale=h_scales[:, i, g, :],
-                        rhs=w_codes[chunk][:, m, g, :].bitcast(FP8X4),
-                        rhs_scale=w_scales[chunk][:, m, g, :],
-                        start=(g == 0),
-                        stop=(g == PASSES - 1),
-                    )
-            scalar_regroup(step + LEAD)
-            silu = ep.tile([P, N_TILE], F32)
-            nc.scalar.activation(out=silu[:], in_=gate_ps[:], func=ACT.Silu)
-            vector_prepare(step + LEAD)
-            g_sb = out_pool.tile([P, N_TILE], F32)
-            nc.vector.tensor_tensor(out=g_sb[:], in0=up_ps[:], in1=silu[:], op=ALU.mult)
+                    for u in range(2):
+                        nc.tensor.transpose(
+                            out=ht[:, g, u, :],
+                            in_=h_words[:, 2 * P * g + u : 2 * P * (g + 1) : 2],
+                            identity=ident_f32[:],
+                        )
+                h_grouped = rows.tile([P, PASSES, P, PACK], BF16, align_bytes=64)
+                nc.scalar.copy(
+                    out=h_grouped[:].rearrange("p g r t -> p (g r t)").bitcast(F32).rearrange(
+                        "q (g r u) -> q g r u", g=PASSES, u=2
+                    ),
+                    in_=ht[:].rearrange("q g u r -> q g r u"),
+                )
+                h_groups[i] = h_grouped
+
+            def quantise_h(i):
+                nc.vector.quantize_mx(
+                    out=h_codes[:, i].rearrange("p g r -> p (g r)").bitcast(FP8X4),
+                    scales=h_scales[:, i].rearrange("p g r -> p (g r)"),
+                    in_=h_groups[i][:].rearrange("p g r t -> p (g r t)"),
+                )
+
+            for i in range(TOKEN_TILES):
+                first_product(i)
+                if i >= 1:
+                    add_and_square(i - 1)
+            for i in range(TOKEN_TILES):
+                norm_and_transpose(i)
+                if i == 0:
+                    add_and_square(TOKEN_TILES - 1)
+                    vector_regroup(0, GATE)
+                    scalar_regroup(0, GATE)
+                    scalar_help(0)
+                if i == 1:
+                    vector_regroup(0, UP)
+                    quantise_h(0)
+                if i >= 2:
+                    vector_prepare(i - 2)
+                    quantise_h(i - 1)
+                if i >= 1:
+                    scalar_prepare(i - 1)
+            quantise_h(TOKEN_TILES - 1)
+            for beat in range(2, LEAD):
+                vector_prepare(beat)
+
+        banks = ctx.enter_context(tc.psum_pool(name="banks", bufs=8))
+        for beat in range(BEATS):
+            chunk = beat // (TOKEN_TILES // BEAT)
+            first_tile = beat % (TOKEN_TILES // BEAT) * BEAT
             first_col = chunk * N_TILE
-            nc.sync.dma_start(
-                out=g_rows[i * P : (i + 1) * P, first_col : first_col + N_TILE], in_=g_sb[:]
-            )
+            products = {}
+            silus = {}
+            for i in range(first_tile, first_tile + BEAT):
+                for m in (GATE, UP):
+                    product = banks.tile([P, N_TILE], F32, tag="bank")
+                    for g in range(PASSES):
+                        nc.tensor.matmul_mx(
+                            out=product[:],
+                            lhsT=h_codes[:, i, g, :].bitcast(FP8X4),
+                            lhsT_scale=h_scales[:, i, g, :],
+                            rhs=w_codes[chunk][:, m, g, :].bitcast(FP8X4),
+                            rhs_scale=w_scales[chunk][:, m, g, :],
+                            start=(g == 0),
+                            stop=(g == PASSES - 1),
+                        )
+                    products[(i, m)] = product
+                silu = ep.tile([P, N_TILE], F32)
+                nc.scalar.activation(out=silu[:], in_=products[(i, GATE)][:], func=ACT.Silu)
+                silus[i] = silu
+            scalar_prepare(beat + LEAD)
+            vector_prepare(beat + LEAD)
+            for i in range(first_tile, first_tile + BEAT):
+                g_sb = out_pool.tile([P, N_TILE], F32)
+                nc.vector.tensor_tensor(
+                    out=g_sb[:], in0=products[(i, UP)][:], in1=silus[i][:], op=ALU.mult
+                )
+                nc.sync.dma_start(
+                    out=g_rows[i * P : (i + 1) * P, first_col : first_col + N_TILE], in_=g_sb[:]
+                )

@@ -30,8 +30,11 @@ BEAT = 2
 BEATS = STEPS // BEAT
 LEAD = 3
 POOL_COLS = 192
-POOL_FIRST = 2
-HELP_COLS = 128
+POOL_FIRST = 5
+HEAD_COLS = 320
+HELP0 = 0
+HELP1 = 64
+HELP_COLS = 96
 RUN = 8
 GATE, UP = 0, 1
 EPS = 1e-6
@@ -104,12 +107,14 @@ def tile_transformerblocktpu_pb_kernel(
                 grouped[(chunk, m, g)] = whole
             return grouped[(chunk, m, g)]
 
-        def pool_cols(chunk):
-            return POOL_COLS if chunk >= POOL_FIRST else 0
+        def pool_cols(chunk, g):
+            return POOL_COLS if 2 * chunk + g >= POOL_FIRST else 0
 
         def vector_regroup(chunk, m):
             if chunk < CHUNKS:
-                first = pool_cols(chunk) + HELP_COLS if m == UP else 0
+                first = pool_cols(chunk, 0) + help_cols(chunk) if m == UP else 0
+                if chunk == 0 and m == GATE:
+                    first = HEAD_COLS
                 regroup(
                     nc.vector.tensor_copy,
                     block(chunk, m, 0, 1 if m == UP else 2)[:, first:, :],
@@ -118,7 +123,7 @@ def tile_transformerblocktpu_pb_kernel(
 
         def scalar_regroup(chunk, m):
             if chunk < CHUNKS:
-                first = pool_cols(chunk) if m == UP else 0
+                first = pool_cols(chunk, 1) if m == UP else 0
                 regroup(
                     nc.scalar.copy,
                     block(chunk, m, 1, 1 if m == UP else 2)[:, first:, :],
@@ -126,16 +131,19 @@ def tile_transformerblocktpu_pb_kernel(
                 )
 
         def scalar_help(chunk):
-            if chunk < CHUNKS:
-                first = pool_cols(chunk)
+            if chunk < CHUNKS and help_cols(chunk):
+                first = pool_cols(chunk, 0)
                 regroup(
                     nc.scalar.copy,
-                    block(chunk, UP, 0, 1)[:, first : first + HELP_COLS, :],
-                    raw_cols(chunk, UP, 0, first, HELP_COLS),
+                    block(chunk, UP, 0, 1)[:, first : first + help_cols(chunk), :],
+                    raw_cols(chunk, UP, 0, first, help_cols(chunk)),
                 )
 
+        def help_cols(chunk):
+            return HELP_COLS if chunk > 1 else (HELP0, HELP1)[chunk]
+
         def pool_regroup(chunk, g):
-            if POOL_FIRST <= chunk < CHUNKS:
+            if chunk < CHUNKS and pool_cols(chunk, g):
                 nc.gpsimd.tensor_scalar(
                     out=block(chunk, UP, g, 1)[:, 0:POOL_COLS, :],
                     in0=raw_cols(chunk, UP, g, 0, POOL_COLS).rearrange("p t n -> p n t"),
@@ -201,10 +209,11 @@ def tile_transformerblocktpu_pb_kernel(
         attn_sb = keep.tile([P, TOKEN_TILES, D_MODEL], BF16)
         for i in range(TOKEN_TILES):
             nc.sync.dma_start(out=attn_sb[:, i, :], in_=attn_rows[i * P : (i + 1) * P, :])
+        load_unit(0)
         x_sb = keep.tile([P, TOKEN_TILES, D_MODEL], BF16)
         for i in range(TOKEN_TILES):
             nc.sync.dma_start(out=x_sb[:, i, :], in_=x_rows[i * P : (i + 1) * P, :])
-        for unit in range(RAW_BUFS):
+        for unit in range(1, RAW_BUFS):
             load_unit(unit)
 
         with ExitStack() as head:
@@ -342,6 +351,9 @@ def tile_transformerblocktpu_pb_kernel(
                     in_=h_groups[i][:].rearrange("p g r t -> p (g r t)"),
                 )
 
+            regroup(
+                nc.scalar.copy, block(0, GATE, 0, 2)[:, 0:HEAD_COLS, :], raw_cols(0, GATE, 0, 0, HEAD_COLS)
+            )
             for i in range(TOKEN_TILES):
                 first_product(i)
                 if i >= 1:

@@ -30,13 +30,16 @@ BEAT = 2
 BEATS = STEPS // BEAT
 LEAD = 3
 POOL_COLS = 192
+POOL_HEAD = 2
 POOL_FIRST = 5
-HEAD_COLS = 320
+XF = 1
+HEAD_COLS = 384
 HELP0 = 0
-HELP1 = 64
-HELP_COLS = 96
+HELP1 = 0
+HELP_COLS = 128
 RUN = 8
 GATE, UP = 0, 1
+TAIL = 256
 EPS = 1e-6
 
 FLOPS = 2 * TOKENS * D_MODEL * (D_MODEL + 2 * D_FF)
@@ -108,7 +111,8 @@ def tile_transformerblocktpu_pb_kernel(
             return grouped[(chunk, m, g)]
 
         def pool_cols(chunk, g):
-            return POOL_COLS if 2 * chunk + g >= POOL_FIRST else 0
+            index = 2 * chunk + g
+            return POOL_COLS if index == POOL_HEAD or index >= POOL_FIRST else 0
 
         def vector_regroup(chunk, m):
             if chunk < CHUNKS:
@@ -171,14 +175,18 @@ def tile_transformerblocktpu_pb_kernel(
             if g == 0:
                 scalar_regroup(chunk, UP)
             else:
-                scalar_help(chunk + 1)
                 scalar_regroup(chunk + 1, GATE)
+
+        def vector_ahead(beat):
+            chunk, g = divmod(beat, 2)
+            vector_regroup(chunk + 1, UP if g else GATE)
 
         def vector_prepare(beat):
             chunk, g = divmod(beat, 2)
             if chunk < CHUNKS:
-                vector_regroup(chunk + 1, UP if g else GATE)
                 quantise_pass(chunk, g)
+                if g == 0:
+                    scalar_help(chunk + 1)
                 pool_regroup(chunk + 1, g)
                 if chunk % 2 == 0 and g == 1:
                     refill(chunk // 2 * 2 * PASSES + RAW_BUFS, 3)
@@ -209,9 +217,10 @@ def tile_transformerblocktpu_pb_kernel(
         attn_sb = keep.tile([P, TOKEN_TILES, D_MODEL], BF16)
         for i in range(TOKEN_TILES):
             nc.sync.dma_start(out=attn_sb[:, i, :], in_=attn_rows[i * P : (i + 1) * P, :])
-        load_unit(0)
         x_sb = keep.tile([P, TOKEN_TILES, D_MODEL], BF16)
         for i in range(TOKEN_TILES):
+            if i == XF:
+                load_unit(0)
             nc.sync.dma_start(out=x_sb[:, i, :], in_=x_rows[i * P : (i + 1) * P, :])
         for unit in range(1, RAW_BUFS):
             load_unit(unit)
@@ -369,45 +378,59 @@ def tile_transformerblocktpu_pb_kernel(
                     vector_regroup(0, UP)
                     quantise_h(0)
                 if i >= 2:
-                    vector_prepare(i - 2)
+                    vector_ahead(i - 2)
                     quantise_h(i - 1)
+                    vector_prepare(i - 2)
                 if i >= 1:
                     scalar_prepare(i - 1)
             quantise_h(TOKEN_TILES - 1)
             for beat in range(2, LEAD):
+                vector_ahead(beat)
                 vector_prepare(beat)
 
         banks = ctx.enter_context(tc.psum_pool(name="banks", bufs=8))
         for beat in range(BEATS):
             chunk = beat // (TOKEN_TILES // BEAT)
             first_tile = beat % (TOKEN_TILES // BEAT) * BEAT
-            first_col = chunk * N_TILE
+            units = [(i, 0, N_TILE) for i in range(first_tile, first_tile + BEAT)]
+            if beat == BEATS - 1:
+                i = first_tile + BEAT - 1
+                units[-1:] = [(i, first, TAIL) for first in range(0, N_TILE, TAIL)]
             products = {}
             silus = {}
-            for i in range(first_tile, first_tile + BEAT):
+            for i, first, width in units:
+                cols = slice(first, first + width)
                 for m in (GATE, UP):
                     product = banks.tile([P, N_TILE], F32, tag="bank")
                     for g in range(PASSES):
                         nc.tensor.matmul_mx(
-                            out=product[:],
+                            out=product[:, 0:width],
                             lhsT=h_codes[:, i, g, :].bitcast(FP8X4),
                             lhsT_scale=h_scales[:, i, g, :],
-                            rhs=w_codes[chunk][:, m, g, :].bitcast(FP8X4),
-                            rhs_scale=w_scales[chunk][:, m, g, :],
+                            rhs=w_codes[chunk][:, m, g, cols].bitcast(FP8X4),
+                            rhs_scale=w_scales[chunk][:, m, g, cols],
                             start=(g == 0),
                             stop=(g == PASSES - 1),
                         )
-                    products[(i, m)] = product
+                    products[(i, first, m)] = product
                 silu = ep.tile([P, N_TILE], F32)
-                nc.scalar.activation(out=silu[:], in_=products[(i, GATE)][:], func=ACT.Silu)
-                silus[i] = silu
+                nc.scalar.activation(
+                    out=silu[:, 0:width], in_=products[(i, first, GATE)][:, 0:width], func=ACT.Silu
+                )
+                silus[(i, first)] = silu
             scalar_prepare(beat + LEAD)
+            vector_ahead(beat + LEAD)
             vector_prepare(beat + LEAD)
-            for i in range(first_tile, first_tile + BEAT):
+            for i, first, width in units:
                 g_sb = out_pool.tile([P, N_TILE], F32)
                 nc.vector.tensor_tensor(
-                    out=g_sb[:], in0=products[(i, UP)][:], in1=silus[i][:], op=ALU.mult
+                    out=g_sb[:, 0:width],
+                    in0=products[(i, first, UP)][:, 0:width],
+                    in1=silus[(i, first)][:, 0:width],
+                    op=ALU.mult,
                 )
+                first_col = chunk * N_TILE + first
                 nc.sync.dma_start(
-                    out=g_rows[i * P : (i + 1) * P, first_col : first_col + N_TILE], in_=g_sb[:]
+                    out=g_rows[i * P : (i + 1) * P, first_col : first_col + width],
+                    in_=g_sb[:, 0:width],
                 )

@@ -36,7 +36,7 @@ XF = 1
 HEAD_COLS = 384
 HELP0 = 0
 HELP1 = 0
-HELP_COLS = 128
+HELP_COLS = 96
 RUN = 8
 GATE, UP = 0, 1
 TAIL = 256
@@ -163,8 +163,8 @@ def tile_transformerblocktpu_pb_kernel(
                 scales = codes_pool.tile([P, 2, PASSES, N_TILE], U8, align_bytes=64)
                 w_codes[chunk] = codes
                 w_scales[chunk] = scales
-            quantise(chunk, GATE, g)
             quantise(chunk, UP, g)
+            quantise(chunk, GATE, g)
 
         def refill(first, count):
             for unit in range(first, min(first + count, UNITS)):

from contextlib import ExitStack

import concourse.mybir as mybir
from concourse.masks import make_identity

F32 = mybir.dt.float32
BF16 = mybir.dt.bfloat16
U32 = mybir.dt.uint32
U8 = mybir.dt.uint8
FP8X4 = mybir.dt.float8_e4m3fn_x4
ACT = mybir.ActivationFunctionType
ALU = mybir.AluOpType

P = 128
PACK = 4
K_PASS = P * PACK
TOKENS = 512
D_MODEL = 1024
D_FF = 4096
TOKEN_TILES = TOKENS // P
PASSES = D_MODEL // K_PASS
N_TILE = 512
HALVES = D_MODEL // N_TILE
CHUNKS = D_FF // N_TILE
STEPS = CHUNKS * TOKEN_TILES
LOAD_COLS = 2 * N_TILE
UNITS = 2 * PASSES * (D_FF // LOAD_COLS)
RAW_BUFS = 9
BEAT = 2
BEATS = STEPS // BEAT
LEAD = 3
POOL_COLS = 192
POOL_HEAD = 2
POOL_FIRST = 5
XF = 1
HEAD_COLS = 384
HELP0 = 0
HELP1 = 0
HELP_COLS = 96
RUN = 8
GATE, UP = 0, 1
TAIL = 256
EPS = 1e-6

FLOPS = 2 * TOKENS * D_MODEL * (D_MODEL + 2 * D_FF)


def regroup(copy, grouped_cols, raw_cols):
    copy(
        out=grouped_cols.rearrange("p (c i) t -> p c t i", i=RUN),
        in_=raw_cols.rearrange("p t (c i) -> p c t i", i=RUN),
    )


def tile_transformerblocktpu_pb_kernel(
    tc, attn, x, w_o, rms2_scale, w_gate, w_up, out_0, out_1
):
    nc = tc.nc
    attn_rows = attn.flatten_outer_dims()
    x_rows = x.flatten_outer_dims()
    xmid_rows = out_0.flatten_outer_dims()
    g_rows = out_1.flatten_outer_dims()

    with ExitStack() as ctx:
        consts = ctx.enter_context(tc.tile_pool(name="consts", bufs=1))
        keep = ctx.enter_context(tc.tile_pool(name="keep", bufs=1))
        raw_pool = ctx.enter_context(tc.tile_pool(name="raw", bufs=RAW_BUFS))
        stage = ctx.enter_context(tc.tile_pool(name="stage", bufs=2))
        rows = ctx.enter_context(tc.tile_pool(name="rows", bufs=2))
        codes_pool = ctx.enter_context(tc.tile_pool(name="codes", bufs=3))
        ep = ctx.enter_context(tc.tile_pool(name="ep", bufs=4))
        out_pool = ctx.enter_context(tc.tile_pool(name="out", bufs=12))
        ctx.enter_context(tc.manual_schedule())

        raws = {}
        grouped = {}
        w_codes = {}
        w_scales = {}

        def load_unit(unit):
            pair, rest = divmod(unit, 2 * PASSES)
            m, g = divmod(rest, PASSES)
            w = (w_gate, w_up)[m]
            raw = raw_pool.tile([P, PACK, LOAD_COLS], BF16, tag="raw")
            nc.sync.dma_start(
                out=raw[:],
                in_=w[
                    g * K_PASS : (g + 1) * K_PASS, pair * LOAD_COLS : (pair + 1) * LOAD_COLS
                ].rearrange("(p t) n -> p t n", t=PACK),
            )
            raws[unit] = raw

        def raw_cols(chunk, m, g, first, width):
            start = (chunk % 2) * N_TILE + first
            unit = (chunk // 2) * 2 * PASSES + m * PASSES + g
            return raws[unit][:, :, start : start + width]

        def quantise(chunk, m, g):
            nc.vector.quantize_mx(
                out=w_codes[chunk][:, m, g, :].bitcast(FP8X4),
                scales=w_scales[chunk][:, m, g, :],
                in_=grouped[(chunk, m, g)][:].rearrange("p n t -> p (n t)"),
            )

        def block(chunk, m, g, bufs):
            if (chunk, m, g) not in grouped:
                whole = stage.tile(
                    [P, N_TILE, PACK], BF16, tag="block%d%d" % (m, g), bufs=bufs, align_bytes=64
                )
                grouped[(chunk, m, g)] = whole
            return grouped[(chunk, m, g)]

        def pool_cols(chunk, g):
            index = 2 * chunk + g
            return POOL_COLS if index == POOL_HEAD or index >= POOL_FIRST else 0

        def vector_regroup(chunk, m):
            if chunk < CHUNKS:
                first = pool_cols(chunk, 0) + help_cols(chunk) if m == UP else 0
                if chunk == 0 and m == GATE:
                    first = HEAD_COLS
                regroup(
                    nc.vector.tensor_copy,
                    block(chunk, m, 0, 1 if m == UP else 2)[:, first:, :],
                    raw_cols(chunk, m, 0, first, N_TILE - first),
                )

        def scalar_regroup(chunk, m):
            if chunk < CHUNKS:
                first = pool_cols(chunk, 1) if m == UP else 0
                regroup(
                    nc.scalar.copy,
                    block(chunk, m, 1, 1 if m == UP else 2)[:, first:, :],
                    raw_cols(chunk, m, 1, first, N_TILE - first),
                )

        def scalar_help(chunk):
            if chunk < CHUNKS and help_cols(chunk):
                first = pool_cols(chunk, 0)
                regroup(
                    nc.scalar.copy,
                    block(chunk, UP, 0, 1)[:, first : first + help_cols(chunk), :],
                    raw_cols(chunk, UP, 0, first, help_cols(chunk)),
                )

        def help_cols(chunk):
            return HELP_COLS if chunk > 1 else (HELP0, HELP1)[chunk]

        def pool_regroup(chunk, g):
            if chunk < CHUNKS and pool_cols(chunk, g):
                nc.gpsimd.tensor_scalar(
                    out=block(chunk, UP, g, 1)[:, 0:POOL_COLS, :],
                    in0=raw_cols(chunk, UP, g, 0, POOL_COLS).rearrange("p t n -> p n t"),
                    scalar1=1.0,
                    scalar2=0.0,
                    op0=ALU.mult,
                    op1=ALU.add,
                )

        def quantise_pass(chunk, g):
            if g == 0:
                codes = codes_pool.tile([P, 2, PASSES, N_TILE], U32, align_bytes=64)
                scales = codes_pool.tile([P, 2, PASSES, N_TILE], U8, align_bytes=64)
                w_codes[chunk] = codes
                w_scales[chunk] = scales
            quantise(chunk, UP, g)
            quantise(chunk, GATE, g)

        def refill(first, count):
            for unit in range(first, min(first + count, UNITS)):
                load_unit(unit)

        def scalar_prepare(beat):
            chunk, g = divmod(beat, 2)
            if g == 0:
                scalar_regroup(chunk, UP)
            else:
                scalar_regroup(chunk + 1, GATE)

        def vector_ahead(beat):
            chunk, g = divmod(beat, 2)
            vector_regroup(chunk + 1, UP if g else GATE)

        def vector_prepare(beat):
            chunk, g = divmod(beat, 2)
            if chunk < CHUNKS:
                quantise_pass(chunk, g)
                if g == 0:
                    scalar_help(chunk + 1)
                pool_regroup(chunk + 1, g)
                if chunk % 2 == 0 and g == 1:
                    refill(chunk // 2 * 2 * PASSES + RAW_BUFS, 3)
                if chunk % 2 == 1 and g == 0:
                    refill(chunk // 2 * 2 * PASSES + RAW_BUFS + 3, 1)

        gain_row = consts.tile([P, D_MODEL], BF16)
        nc.vector.memset(gain_row[:], 0.0)
        neg_half = consts.tile([P, 1], F32)
        nc.vector.memset(neg_half[:], -0.5)
        ones = consts.tile([P, P], BF16)
        nc.vector.memset(ones[:], 1.0)
        warm = consts.tile([P, 1], F32)
        nc.scalar.activation(out=warm[:], in_=neg_half[:], func=ACT.Silu)
        ident_f32 = consts.tile([P, P], F32)
        make_identity(nc, ident_f32[:])

        wo_raw = []
        for g in range(PASSES):
            raw = raw_pool.tile([P, PACK, LOAD_COLS], BF16, tag="raw")
            nc.sync.dma_start(
                out=raw[:],
                in_=w_o[g * K_PASS : (g + 1) * K_PASS, :].rearrange("(p t) n -> p t n", t=PACK),
            )
            wo_raw.append(raw)
            if g == 0:
                nc.sync.dma_start(out=gain_row[0:1, :], in_=rms2_scale.unsqueeze(0))
        attn_sb = keep.tile([P, TOKEN_TILES, D_MODEL], BF16)
        for i in range(TOKEN_TILES):
            nc.sync.dma_start(out=attn_sb[:, i, :], in_=attn_rows[i * P : (i + 1) * P, :])
        x_sb = keep.tile([P, TOKEN_TILES, D_MODEL], BF16)
        for i in range(TOKEN_TILES):
            if i == XF:
                load_unit(0)
            nc.sync.dma_start(out=x_sb[:, i, :], in_=x_rows[i * P : (i + 1) * P, :])
        for unit in range(1, RAW_BUFS):
            load_unit(unit)

        with ExitStack() as head:
            head_banks = head.enter_context(tc.psum_pool(name="head_banks", bufs=7))
            gain_bank = head.enter_context(tc.psum_pool(name="gain_bank", bufs=1))
            gain_ps = gain_bank.tile([P, D_MODEL], BF16)
            for half in range(HALVES):
                nc.tensor.matmul(
                    out=gain_ps[:, half * N_TILE : (half + 1) * N_TILE],
                    lhsT=ones[:],
                    rhs=gain_row[:, half * N_TILE : (half + 1) * N_TILE],
                    start=True,
                    stop=True,
                )

            wo_codes = keep.tile([P, PASSES, D_MODEL], U32, align_bytes=64)
            wo_scales = keep.tile([P, PASSES, D_MODEL], U8, align_bytes=64)
            for g in range(PASSES):
                by_vector = stage.tile([P, N_TILE, PACK], BF16, tag="block00", align_bytes=64)
                regroup(nc.vector.tensor_copy, by_vector[:], wo_raw[g][:, :, 0:N_TILE])
                by_scalar = stage.tile([P, N_TILE, PACK], BF16, tag="block01", align_bytes=64)
                regroup(nc.scalar.copy, by_scalar[:], wo_raw[g][:, :, N_TILE : 2 * N_TILE])
                for half, tile_ in enumerate((by_vector, by_scalar)):
                    cols = slice(half * N_TILE, (half + 1) * N_TILE)
                    nc.vector.quantize_mx(
                        out=wo_codes[:, g, cols].bitcast(FP8X4),
                        scales=wo_scales[:, g, cols],
                        in_=tile_[:].rearrange("p n t -> p (n t)"),
                    )

            a_grouped = keep.tile([P, TOKEN_TILES, PASSES, P, PACK], BF16, align_bytes=64)
            a_codes = keep.tile([P, TOKEN_TILES, PASSES, P], U32, align_bytes=64)
            a_scales = keep.tile([P, TOKEN_TILES, PASSES, P], U8, align_bytes=64)
            for i in range(TOKEN_TILES):
                attn_words = attn_sb[:, i, :].bitcast(F32)
                at = head_banks.tile([P, PASSES, 2, P], F32, tag="bank")
                for g in range(PASSES):
                    for u in range(2):
                        nc.tensor.transpose(
                            out=at[:, g, u, :],
                            in_=attn_words[:, 2 * P * g + u : 2 * P * (g + 1) : 2],
                            identity=ident_f32[:],
                        )
                nc.scalar.copy(
                    out=a_grouped[:, i].bitcast(F32),
                    in_=at[:].rearrange("q g u r -> q g r u"),
                )
                nc.vector.quantize_mx(
                    out=a_codes[:, i].rearrange("q g r -> q (g r)").bitcast(FP8X4),
                    scales=a_scales[:, i].rearrange("q g r -> q (g r)"),
                    in_=a_grouped[:, i].rearrange("q g r t -> q (g r t)"),
                )

            xmid = keep.tile([P, TOKEN_TILES, D_MODEL], F32)
            sumsq = keep.tile([P, TOKEN_TILES], F32)
            shifted = keep.tile([P, TOKEN_TILES], F32)
            inv_norm = keep.tile([P, TOKEN_TILES], F32)
            h_codes = keep.tile([P, TOKEN_TILES, PASSES, P], U32, align_bytes=64)
            h_scales = keep.tile([P, TOKEN_TILES, PASSES, P], U8, align_bytes=64)
            xm_banks = {}
            h_groups = {}

            def first_product(i):
                for half in range(HALVES):
                    cols = slice(half * N_TILE, (half + 1) * N_TILE)
                    xm_ps = head_banks.tile([P, N_TILE], F32, tag="bank")
                    for g in range(PASSES):
                        nc.tensor.matmul_mx(
                            out=xm_ps[:],
                            lhsT=a_codes[:, i, g, :].bitcast(FP8X4),
                            lhsT_scale=a_scales[:, i, g, :],
                            rhs=wo_codes[:, g, cols].bitcast(FP8X4),
                            rhs_scale=wo_scales[:, g, cols],
                            start=(g == 0),
                            stop=(g == PASSES - 1),
                        )
                    xm_banks[(i, half)] = xm_ps

            def add_and_square(i):
                one = slice(i, i + 1)
                for half in range(HALVES):
                    cols = slice(half * N_TILE, (half + 1) * N_TILE)
                    nc.vector.tensor_tensor(
                        out=xmid[:, i, cols], in0=xm_banks[(i, half)][:], in1=x_sb[:, i, cols], op=ALU.add
                    )
                nc.sync.dma_start(out=xmid_rows[i * P : (i + 1) * P, :], in_=xmid[:, i, :])
                squares = rows.tile([P, D_MODEL], BF16)
                nc.scalar.activation(
                    out=squares[:], in_=xmid[:, i, :], func=ACT.Square, accum_out=sumsq[:, one]
                )
                nc.gpsimd.tensor_scalar(
                    out=shifted[:, one],
                    in0=sumsq[:, one],
                    scalar1=D_MODEL * EPS,
                    scalar2=1.0 / D_MODEL,
                    op0=ALU.add,
                    op1=ALU.mult,
                )
                nc.gpsimd.tensor_tensor(
                    out=inv_norm[:, one], in0=shifted[:, one], in1=neg_half[:], op=ALU.pow
                )

            def norm_and_transpose(i):
                h_bf16 = rows.tile([P, D_MODEL], BF16)
                nc.vector.scalar_tensor_tensor(
                    out=h_bf16[:],
                    in0=xmid[:, i, :],
                    scalar=inv_norm[:, i : i + 1],
                    in1=gain_ps[:],
                    op0=ALU.mult,
                    op1=ALU.mult,
                )
                h_words = h_bf16[:].bitcast(F32)
                ht = head_banks.tile([P, PASSES, 2, P], F32, tag="bank")
                for g in range(PASSES):
                    for u in range(2):
                        nc.tensor.transpose(
                            out=ht[:, g, u, :],
                            in_=h_words[:, 2 * P * g + u : 2 * P * (g + 1) : 2],
                            identity=ident_f32[:],
                        )
                h_grouped = rows.tile([P, PASSES, P, PACK], BF16, align_bytes=64)
                nc.scalar.copy(
                    out=h_grouped[:].rearrange("p g r t -> p (g r t)").bitcast(F32).rearrange(
                        "q (g r u) -> q g r u", g=PASSES, u=2
                    ),
                    in_=ht[:].rearrange("q g u r -> q g r u"),
                )
                h_groups[i] = h_grouped

            def quantise_h(i):
                nc.vector.quantize_mx(
                    out=h_codes[:, i].rearrange("p g r -> p (g r)").bitcast(FP8X4),
                    scales=h_scales[:, i].rearrange("p g r -> p (g r)"),
                    in_=h_groups[i][:].rearrange("p g r t -> p (g r t)"),
                )

            regroup(
                nc.scalar.copy, block(0, GATE, 0, 2)[:, 0:HEAD_COLS, :], raw_cols(0, GATE, 0, 0, HEAD_COLS)
            )
            for i in range(TOKEN_TILES):
                first_product(i)
                if i >= 1:
                    add_and_square(i - 1)
            for i in range(TOKEN_TILES):
                norm_and_transpose(i)
                if i == 0:
                    add_and_square(TOKEN_TILES - 1)
                    vector_regroup(0, GATE)
                    scalar_regroup(0, GATE)
                    scalar_help(0)
                if i == 1:
                    vector_regroup(0, UP)
                    quantise_h(0)
                if i >= 2:
                    vector_ahead(i - 2)
                    quantise_h(i - 1)
                    vector_prepare(i - 2)
                if i >= 1:
                    scalar_prepare(i - 1)
            quantise_h(TOKEN_TILES - 1)
            for beat in range(2, LEAD):
                vector_ahead(beat)
                vector_prepare(beat)

        banks = ctx.enter_context(tc.psum_pool(name="banks", bufs=8))
        for beat in range(BEATS):
            chunk = beat // (TOKEN_TILES // BEAT)
            first_tile = beat % (TOKEN_TILES // BEAT) * BEAT
            units = [(i, 0, N_TILE) for i in range(first_tile, first_tile + BEAT)]
            if beat == BEATS - 1:
                i = first_tile + BEAT - 1
                units[-1:] = [(i, first, TAIL) for first in range(0, N_TILE, TAIL)]
            products = {}
            silus = {}
            for i, first, width in units:
                cols = slice(first, first + width)
                for m in (GATE, UP):
                    product = banks.tile([P, N_TILE], F32, tag="bank")
                    for g in range(PASSES):
                        nc.tensor.matmul_mx(
                            out=product[:, 0:width],
                            lhsT=h_codes[:, i, g, :].bitcast(FP8X4),
                            lhsT_scale=h_scales[:, i, g, :],
                            rhs=w_codes[chunk][:, m, g, cols].bitcast(FP8X4),
                            rhs_scale=w_scales[chunk][:, m, g, cols],
                            start=(g == 0),
                            stop=(g == PASSES - 1),
                        )
                    products[(i, first, m)] = product
                silu = ep.tile([P, N_TILE], F32)
                nc.scalar.activation(
                    out=silu[:, 0:width], in_=products[(i, first, GATE)][:, 0:width], func=ACT.Silu
                )
                silus[(i, first)] = silu
            scalar_prepare(beat + LEAD)
            vector_ahead(beat + LEAD)
            vector_prepare(beat + LEAD)
            for i, first, width in units:
                g_sb = out_pool.tile([P, N_TILE], F32)
                nc.vector.tensor_tensor(
                    out=g_sb[:, 0:width],
                    in0=products[(i, first, UP)][:, 0:width],
                    in1=silus[(i, first)][:, 0:width],
                    op=ALU.mult,
                )
                first_col = chunk * N_TILE + first
                nc.sync.dma_start(
                    out=g_rows[i * P : (i + 1) * P, first_col : first_col + width],
                    in_=g_sb[:, 0:width],
                )
